import numpy as np
import ml_dtypes


BF16 = ml_dtypes.bfloat16


def bf(x):
    return np.asarray(x, np.float32).astype(BF16)


def f64(x):
    return np.asarray(x).astype(np.float64)


E2M1 = np.array([0.0, 0.5, 1.0, 1.5, 2.0, 3.0, 4.0, 6.0, -0.0, -0.5, -1.0, -1.5, -2.0, -3.0, -4.0, -6.0])


def pack_weight(w, fmt):
    k, n = w.shape
    w = f64(bf(w)).reshape(k // 32, 32, n)
    amax = np.abs(w).max(1)
    if fmt == "e4m3":
        byte = np.frexp(amax)[1] - 1 + 127 - 7
    else:
        mant, ex = np.frexp(amax / 6.0)
        byte = np.where(mant > 0.5, ex, ex - 1) + 127
    byte = np.clip(np.where(amax > 0, byte, 1), 1, 254)
    scaled = (w * np.exp2(127.0 - byte)[:, None, :]).reshape(k, n).astype(np.float32)
    by_word = np.ascontiguousarray(scaled.reshape(k // 512, 128, 4, n).transpose(0, 1, 3, 2))
    if fmt == "e4m3":
        words = by_word.astype(ml_dtypes.float8_e4m3fn).view(np.uint8)
    else:
        c = by_word.astype(ml_dtypes.float4_e2m1fn).view(np.uint8) & 0xF
        words = c[..., 0::2] | (c[..., 1::2] << 4)
    return np.ascontiguousarray(words), np.ascontiguousarray(byte.astype(np.uint8).reshape(k // 512, 16, n))


def unpack_weight(words, scales, fmt):
    g, p, n, _ = words.shape
    if fmt == "e4m3":
        vals = np.ascontiguousarray(words).view(ml_dtypes.float8_e4m3fn).astype(np.float64)
    else:
        nib = np.empty((g, p, n, 4), np.uint8)
        nib[..., 0::2] = words & 0xF
        nib[..., 1::2] = words >> 4
        vals = E2M1[nib]
    vals = vals * np.repeat(np.exp2(scales.astype(np.float64) - 127.0), 8, axis=1)[..., None]
    return vals.transpose(0, 1, 3, 2).reshape(g * 512, n)

def pack4(w):
    words, scales = pack_weight(w, "e2m1")
    return words.reshape(words.shape[0], 128, -1), scales


def unpack4(words, scales):
    return unpack_weight(words.reshape(words.shape[0], 128, -1, 2), scales, "e2m1")


def kspread(k):
    return np.exp2(np.repeat(np.random.randint(-6, 7, k // 32), 32).astype(np.float64))


B, S, D, NH, NKV, HD = 1, 512, 2048, 16, 4, 128
ROPE_THETA = 10000.0


def rope_tables():
    freqs = 1.0 / (ROPE_THETA ** (f64(np.arange(0, HD, 2)) / HD))
    ang = np.outer(f64(np.arange(S)), freqs)
    return np.cos(ang), np.sin(ang)


def rope(x, cos, sin):
    xr = x.reshape(*x.shape[:-1], HD // 2, 2)
    re, im = xr[..., 0], xr[..., 1]
    c = cos[None, :, None, :]
    s = sin[None, :, None, :]
    return np.stack((re * c - im * s, re * s + im * c), axis=-1).reshape(x.shape)


def setup_inputs():
    s = kspread(D)
    hidden_states = np.random.standard_normal((B, S, D)) * s
    hidden_states_words, hidden_states_scales = pack4(hidden_states.reshape(B * S, D).T)
    wq_words, wq_scales = pack4(np.random.standard_normal((D, NH * HD)) / np.sqrt(D) / s[:, None])
    wk_words, wk_scales = pack4(np.random.standard_normal((D, NKV * HD)) / np.sqrt(D) / s[:, None])
    wv_words, wv_scales = pack4(np.random.standard_normal((D, NKV * HD)) * 2.0 / np.sqrt(D) / s[:, None])
    return {"hidden_states_words": hidden_states_words, "hidden_states_scales": hidden_states_scales,
            "wq_words": wq_words, "wq_scales": wq_scales,
            "wk_words": wk_words, "wk_scales": wk_scales,
            "wv_words": wv_words, "wv_scales": wv_scales}


def reference(hidden_states_words, hidden_states_scales, wq_words, wq_scales, wk_words, wk_scales, wv_words, wv_scales):
    xq = unpack4(hidden_states_words, hidden_states_scales).T.reshape(B, S, D)
    q = (xq @ unpack4(wq_words, wq_scales)).reshape(B, S, NH, HD)
    k = (xq @ unpack4(wk_words, wk_scales)).reshape(B, S, NKV, HD)
    v = (xq @ unpack4(wv_words, wv_scales)).reshape(B, S, NKV, HD)
    cos, sin = rope_tables()
    return rope(q, cos, sin), rope(k, cos, sin), v

@@ -1,0 +1,254 @@
+import math
+from contextlib import ExitStack
+
+import concourse.mybir as mybir
+
+FLOPS = 2 * 512 * 2048 * 3072
+
+F32 = mybir.dt.float32
+BF16 = mybir.dt.bfloat16
+I32 = mybir.dt.int32
+U8 = mybir.dt.uint8
+FP4X4 = mybir.dt.float4_e2m1fn_x4
+ALU = mybir.AluOpType
+ACTF = mybir.ActivationFunctionType
+
+P = 128
+PASSES = 4
+TOKEN_TILES = 4
+BLOCK = 512
+HEAD = 128
+PAIRS = HEAD // 2
+ROPE_THETA = 10000.0
+TWO_PI = 2.0 * math.pi
+WARM_MATMULS = 10
+VECTOR_ADD_EVERY = 5
+
+
+def tile_rptattention_pa_kernel(
+    tc,
+    hidden_states_words,
+    hidden_states_scales,
+    wq_words,
+    wq_scales,
+    wk_words,
+    wk_scales,
+    wv_words,
+    wv_scales,
+    out_0,
+    out_1,
+    out_2,
+):
+    nc = tc.nc
+    q_out = out_0.rearrange("b s h d -> (b s) (h d)")
+    k_out = out_1.rearrange("b s h d -> (b s) (h d)")
+    v_out = out_2.rearrange("b s h d -> (b s) (h d)")
+
+    units = [
+        (wq_words, wq_scales, 0, BLOCK),
+        (wq_words, wq_scales, BLOCK, BLOCK),
+        (wq_words, wq_scales, 2 * BLOCK, 2 * BLOCK),
+        (wk_words, wk_scales, 0, BLOCK),
+        (wv_words, wv_scales, 0, BLOCK),
+    ]
+    blocks = [
+        (0, 0, q_out, 0, True),
+        (1, 0, q_out, BLOCK, True),
+        (2, 0, q_out, 2 * BLOCK, True),
+        (2, BLOCK, q_out, 3 * BLOCK, True),
+        (3, 0, k_out, 0, True),
+        (4, 0, v_out, 0, False),
+    ]
+
+    with ExitStack() as ctx:
+        keep = ctx.enter_context(tc.tile_pool(name="keep", bufs=1))
+        work = ctx.enter_context(tc.tile_pool(name="work", bufs=6))
+        psum = ctx.enter_context(tc.psum_pool(name="psum", bufs=8))
+
+        warm_bf = keep.tile([P, P + BLOCK], BF16, name="warm_bf")
+        nc.gpsimd.memset(warm_bf[:], 0.0)
+        warm_in = keep.tile([P, 1], F32, name="warm_in")
+        warm_out = keep.tile([P, 1], F32, name="warm_out")
+        nc.gpsimd.memset(warm_in[:], 0.0)
+        nc.scalar.activation(out=warm_out[:], in_=warm_in[:], func=ACTF.Sin)
+        warm_acc = psum.tile([P, BLOCK], F32, name="acc")
+        for i in range(WARM_MATMULS):
+            nc.tensor.matmul(out=warm_acc[:], lhsT=warm_bf[:, 0:P], rhs=warm_bf[:, P : P + BLOCK], start=True, stop=True)
+
+        x_codes = keep.tile([P, PASSES, 2 * BLOCK], U8, name="x_codes", align_bytes=64)
+        x_planes = keep.tile([P, PASSES, BLOCK], U8, name="x_planes", align_bytes=64)
+        w_codes = []
+        w_planes = []
+        for u in range(len(units)):
+            cols = units[u][3]
+            wc = keep.tile([P, PASSES, 2 * cols], U8, name="w_codes%d" % u, align_bytes=64)
+            wp = keep.tile([P, PASSES, cols], U8, name="w_planes%d" % u, align_bytes=64)
+            w_codes.append(wc)
+            w_planes.append(wp)
+
+        def load_scales(planes, scales, c0, cols):
+            for q in range(4):
+                nc.sync.dma_start(
+                    out=planes[32 * q : 32 * q + 4, :, :].bitcast(I32),
+                    in_=scales[:, 4 * q : 4 * q + 4, c0 : c0 + cols].rearrange("g r n -> r g n").bitcast(I32),
+                )
+
+        def load_unit_scales(u):
+            load_scales(w_planes[u], units[u][1], units[u][2], units[u][3])
+
+        def load_unit_codes(u):
+            words, c0, cols = units[u][0], units[u][2], units[u][3]
+            nc.sync.dma_start(
+                out=w_codes[u][:].bitcast(I32),
+                in_=words[:, :, 2 * c0 : 2 * (c0 + cols)].rearrange("g p c -> p g c").bitcast(I32),
+            )
+
+        def load_first_codes(g):
+            nc.sync.dma_start(out=x_codes[:, g, :].bitcast(I32), in_=hidden_states_words[g].bitcast(I32))
+            nc.sync.dma_start(out=w_codes[0][:, g, :].bitcast(I32), in_=wq_words[g][:, 0 : 2 * BLOCK].bitcast(I32))
+
+        nc.vector.memset(x_planes[:].bitcast(I32), 0)
+        nc.vector.memset(w_planes[0][:].bitcast(I32), 0)
+        load_first_codes(0)
+        load_scales(x_planes, hidden_states_scales, 0, BLOCK)
+        load_unit_scales(0)
+        for g in range(1, PASSES):
+            load_first_codes(g)
+
+        pos_i = keep.tile([P, TOKEN_TILES], I32, name="pos_i")
+        nc.gpsimd.iota(out=pos_i[:], pattern=[[P, TOKEN_TILES]], base=0, channel_multiplier=1)
+        freq = keep.tile([P, PAIRS], F32, name="freq")
+        nc.gpsimd.memset(freq[:, 0:1], 1.0)
+        ratio = ROPE_THETA ** (-2.0 / HEAD)
+        s = 1
+        while s < PAIRS:
+            nc.gpsimd.tensor_scalar(
+                out=freq[:, s : 2 * s], in0=freq[:, 0:s], scalar1=ratio**s, scalar2=1.0, op0=ALU.mult, op1=ALU.mult
+            )
+            s *= 2
+        sign = keep.tile([P, PAIRS, 2], F32, name="sign")
+        nc.gpsimd.memset(sign[:], 1.0)
+        nc.gpsimd.memset(sign[:, :, 0:1], -1.0)
+        for u in range(2, len(units)):
+            nc.gpsimd.memset(w_planes[u][:].bitcast(F32), 0.0)
+
+        pos_f = keep.tile([P, TOKEN_TILES], F32, name="pos_f")
+        nc.vector.tensor_copy(out=pos_f[:], in_=pos_i[:])
+        turns = keep.tile([P, 2, TOKEN_TILES, PAIRS], F32, name="turns")
+        for t in range(TOKEN_TILES):
+            nc.vector.tensor_scalar(
+                out=turns[:, 0, t, :],
+                in0=freq[:],
+                scalar1=pos_f[:, t : t + 1],
+                scalar2=1.0 / TWO_PI,
+                op0=ALU.mult,
+                op1=ALU.mult,
+            )
+        nc.vector.tensor_scalar(
+            out=turns[:, 1, :, :], in0=turns[:, 0, :, :], scalar1=0.25, scalar2=None, op0=ALU.add
+        )
+        whole = keep.tile([P, 2, TOKEN_TILES, PAIRS], I32, name="whole")
+        nc.vector.tensor_copy(out=whole[:], in_=turns[:])
+        frac = keep.tile([P, 2, TOKEN_TILES, PAIRS], F32, name="frac")
+        nc.vector.tensor_tensor(out=frac[:], in0=turns[:], in1=whole[:], op=ALU.subtract)
+        neg_frac = keep.tile([P, 2, TOKEN_TILES, PAIRS], F32, name="neg_frac")
+        nc.vector.scalar_tensor_tensor(
+            out=neg_frac[:].rearrange("p a t j -> p (a t j)"),
+            in0=frac[:].rearrange("p a t j -> p (a t j)"),
+            scalar=0.5,
+            in1=frac[:].rearrange("p a t j -> p (a t j)"),
+            op0=ALU.is_gt,
+            op1=ALU.subtract,
+        )
+        nc.vector.memset(w_planes[1][:].bitcast(I32), 0)
+
+        load_unit_scales(1)
+        load_unit_codes(1)
+        for u in range(2, len(units)):
+            load_unit_scales(u)
+        for u in range(2, len(units)):
+            load_unit_codes(u)
+
+        sin_cos = keep.tile([P, 2, TOKEN_TILES, PAIRS], F32, name="sin_cos")
+        nc.scalar.activation(out=sin_cos[:], in_=neg_frac[:], func=ACTF.Sin, scale=-TWO_PI)
+        full = [P, TOKEN_TILES, PAIRS, 2]
+        cos_tab = keep.tile(full, F32, name="cos_tab")
+        sin_tab = keep.tile(full, F32, name="sin_tab")
+        nc.vector.tensor_copy(out=cos_tab[:], in_=sin_cos[:, 1, :, :].unsqueeze(3).to_broadcast(full))
+        nc.vector.tensor_tensor(
+            out=sin_tab[:],
+            in0=sin_cos[:, 0, :, :].unsqueeze(3).to_broadcast(full),
+            in1=sign[:].unsqueeze(1).to_broadcast(full),
+            op=ALU.mult,
+        )
+
+        def one_pass(acc, n, m, g, first=0, cols=BLOCK):
+            u, c0 = blocks[n][0], blocks[n][1] + first
+            nc.tensor.matmul_mx(
+                out=acc[:],
+                lhsT=x_codes[:, g, 2 * P * m : 2 * P * (m + 1)].bitcast(FP4X4),
+                lhsT_scale=x_planes[:, g, P * m : P * (m + 1)],
+                rhs=w_codes[u][:, g, 2 * c0 : 2 * (c0 + cols)].bitcast(FP4X4),
+                rhs_scale=w_planes[u][:, g, c0 : c0 + cols],
+                start=(g == 0),
+                stop=(g == PASSES - 1),
+            )
+
+        def rope(acc, n, m, index):
+            out_view, oc0 = blocks[n][2], blocks[n][3]
+            heads = BLOCK // HEAD
+            by_head = [P, heads, PAIRS, 2]
+            y = work.tile([P, BLOCK], F32, name="y")
+            t1 = work.tile([P, BLOCK], F32, name="t1")
+            t2 = work.tile([P, BLOCK], F32, name="t2")
+            pairs = acc[:].rearrange("p (h j e) -> p h j e", h=heads, e=2)
+            nc.vector.tensor_tensor(
+                out=t1[:].rearrange("p (h j e) -> p h j e", h=heads, e=2),
+                in0=pairs,
+                in1=cos_tab[:, m, :, :].unsqueeze(1).to_broadcast(by_head),
+                op=ALU.mult,
+            )
+            nc.vector.tensor_tensor(
+                out=t2[:].rearrange("p (h j e) -> p h j e", h=heads, e=2),
+                in0=pairs[:, :, :, ::-1],
+                in1=sin_tab[:, m, :, :].unsqueeze(1).to_broadcast(by_head),
+                op=ALU.mult,
+            )
+            if index % VECTOR_ADD_EVERY == VECTOR_ADD_EVERY - 1:
+                nc.vector.tensor_tensor(out=y[:], in0=t1[:], in1=t2[:], op=ALU.add)
+            else:
+                nc.gpsimd.tensor_tensor(out=y[:], in0=t1[:], in1=t2[:], op=ALU.add)
+            nc.sync.dma_start(out=out_view[P * m : P * (m + 1), oc0 : oc0 + BLOCK], in_=y[:])
+
+        def plain(acc, n, m, first=0, cols=BLOCK):
+            out_view, oc0 = blocks[n][2], blocks[n][3] + first
+            v = work.tile([P, cols], F32, name="v", bufs=4)
+            nc.scalar.copy(out=v[:], in_=acc[:])
+            nc.scalar.dma_start(out=out_view[P * m : P * (m + 1), oc0 : oc0 + cols], in_=v[:])
+
+        groups = [(n, m) for n in range(len(blocks)) for m in range(TOKEN_TILES)]
+        index = 0
+        acc_a = psum.tile([P, BLOCK], F32, name="acc")
+        acc_b = psum.tile([P, BLOCK], F32, name="acc")
+        for g in range(PASSES):
+            one_pass(acc_a, 0, 0, g)
+            one_pass(acc_b, 0, 1, g)
+        rope(acc_a, 0, 0, 0)
+        rope(acc_b, 0, 1, 1)
+        index = 2
+        for n, m in groups[index:-1]:
+            acc = psum.tile([P, BLOCK], F32, name="acc")
+            for g in range(PASSES):
+                one_pass(acc, n, m, g)
+            if blocks[n][4]:
+                rope(acc, n, m, index)
+            else:
+                plain(acc, n, m)
+            index += 1
+        n, m = groups[-1]
+        half = BLOCK // 2
+        for first in (0, half):
+            acc = psum.tile([P, half], F32, name="acc")
+            for g in range(PASSES):
+                one_pass(acc, n, m, g, first, half)
+            plain(acc, n, m, first, half)

@@ -19,10 +19,11 @@ TOKEN_TILES = 4
 BLOCK = 512
 HEAD = 128
 PAIRS = HEAD // 2
+HEADS = BLOCK // HEAD
 ROPE_THETA = 10000.0
 TWO_PI = 2.0 * math.pi
-WARM_MATMULS = 10
-VECTOR_ADD_EVERY = 5
+WARM_MATMULS = 12
+EARLY_STORES = 5
 
 
 def tile_rptattention_pa_kernel(
@@ -51,18 +52,18 @@ def tile_rptattention_pa_kernel(
         (wk_words, wk_scales, 0, BLOCK),
         (wv_words, wv_scales, 0, BLOCK),
     ]
-    blocks = [
-        (0, 0, q_out, 0, True),
-        (1, 0, q_out, BLOCK, True),
-        (2, 0, q_out, 2 * BLOCK, True),
-        (2, BLOCK, q_out, 3 * BLOCK, True),
-        (3, 0, k_out, 0, True),
-        (4, 0, v_out, 0, False),
+    rope_blocks = [
+        (0, 0, q_out, 0),
+        (1, 0, q_out, BLOCK),
+        (2, 0, q_out, 2 * BLOCK),
+        (2, BLOCK, q_out, 3 * BLOCK),
+        (3, 0, k_out, 0),
     ]
+    v_block = (4, 0, v_out, 0)
 
     with ExitStack() as ctx:
         keep = ctx.enter_context(tc.tile_pool(name="keep", bufs=1))
-        work = ctx.enter_context(tc.tile_pool(name="work", bufs=6))
+        work = ctx.enter_context(tc.tile_pool(name="work", bufs=5))
         psum = ctx.enter_context(tc.psum_pool(name="psum", bufs=8))
 
         warm_bf = keep.tile([P, P + BLOCK], BF16, name="warm_bf")
@@ -86,15 +87,18 @@ def tile_rptattention_pa_kernel(
             w_codes.append(wc)
             w_planes.append(wp)
 
-        def load_scales(planes, scales, c0, cols):
-            for q in range(4):
-                nc.sync.dma_start(
-                    out=planes[32 * q : 32 * q + 4, :, :].bitcast(I32),
-                    in_=scales[:, 4 * q : 4 * q + 4, c0 : c0 + cols].rearrange("g r n -> r g n").bitcast(I32),
-                )
+        def load_scale_quadrant(planes, scales, c0, cols, q):
+            nc.sync.dma_start(
+                out=planes[32 * q : 32 * q + 4, :, :].bitcast(I32),
+                in_=scales[:, 4 * q : 4 * q + 4, c0 : c0 + cols].rearrange("g r n -> r g n").bitcast(I32),
+            )
 
-        def load_unit_scales(u):
-            load_scales(w_planes[u], units[u][1], units[u][2], units[u][3])
+        def load_x_scales(q):
+            load_scale_quadrant(x_planes, hidden_states_scales, 0, BLOCK, q)
+
+        def load_unit_scales(u, quadrants=(0, 1, 2, 3)):
+            for q in quadrants:
+                load_scale_quadrant(w_planes[u], units[u][1], units[u][2], units[u][3], q)
 
         def load_unit_codes(u):
             words, c0, cols = units[u][0], units[u][2], units[u][3]
@@ -103,17 +107,23 @@ def tile_rptattention_pa_kernel(
                 in_=words[:, :, 2 * c0 : 2 * (c0 + cols)].rearrange("g p c -> p g c").bitcast(I32),
             )
 
-        def load_first_codes(g):
-            nc.sync.dma_start(out=x_codes[:, g, :].bitcast(I32), in_=hidden_states_words[g].bitcast(I32))
-            nc.sync.dma_start(out=w_codes[0][:, g, :].bitcast(I32), in_=wq_words[g][:, 0 : 2 * BLOCK].bitcast(I32))
+        def load_first_codes(g0, g1):
+            nc.sync.dma_start(
+                out=x_codes[:, g0:g1, :].bitcast(I32),
+                in_=hidden_states_words[g0:g1].rearrange("g p c -> p g c").bitcast(I32),
+            )
+            nc.sync.dma_start(
+                out=w_codes[0][:, g0:g1, :].bitcast(I32),
+                in_=wq_words[g0:g1, :, 0 : 2 * BLOCK].rearrange("g p c -> p g c").bitcast(I32),
+            )
 
         nc.vector.memset(x_planes[:].bitcast(I32), 0)
         nc.vector.memset(w_planes[0][:].bitcast(I32), 0)
-        load_first_codes(0)
-        load_scales(x_planes, hidden_states_scales, 0, BLOCK)
+        load_first_codes(0, 1)
+        for q in range(4):
+            load_x_scales(q)
         load_unit_scales(0)
-        for g in range(1, PASSES):
-            load_first_codes(g)
+        load_first_codes(1, PASSES)
 
         pos_i = keep.tile([P, TOKEN_TILES], I32, name="pos_i")
         nc.gpsimd.iota(out=pos_i[:], pattern=[[P, TOKEN_TILES]], base=0, channel_multiplier=1)
@@ -164,10 +174,12 @@ def tile_rptattention_pa_kernel(
 
         load_unit_scales(1)
         load_unit_codes(1)
-        for u in range(2, len(units)):
-            load_unit_scales(u)
-        for u in range(2, len(units)):
-            load_unit_codes(u)
+        load_unit_scales(2)
+        load_unit_codes(2)
+        load_unit_scales(3)
+        load_unit_scales(4)
+        load_unit_codes(3)
+        load_unit_codes(4)
 
         sin_cos = keep.tile([P, 2, TOKEN_TILES, PAIRS], F32, name="sin_cos")
         nc.scalar.activation(out=sin_cos[:], in_=neg_frac[:], func=ACTF.Sin, scale=-TWO_PI)
@@ -182,73 +194,75 @@ def tile_rptattention_pa_kernel(
             op=ALU.mult,
         )
 
-        def one_pass(acc, n, m, g, first=0, cols=BLOCK):
-            u, c0 = blocks[n][0], blocks[n][1] + first
-            nc.tensor.matmul_mx(
-                out=acc[:],
-                lhsT=x_codes[:, g, 2 * P * m : 2 * P * (m + 1)].bitcast(FP4X4),
-                lhsT_scale=x_planes[:, g, P * m : P * (m + 1)],
-                rhs=w_codes[u][:, g, 2 * c0 : 2 * (c0 + cols)].bitcast(FP4X4),
-                rhs_scale=w_planes[u][:, g, c0 : c0 + cols],
-                start=(g == 0),
-                stop=(g == PASSES - 1),
+        by_head = [P, HEADS, PAIRS, 2]
+
+        def group(block, m, first=0, cols=BLOCK):
+            u, c0 = block[0], block[1] + first
+            acc = psum.tile([P, cols], F32, name="acc")
+            for g in range(PASSES):
+                nc.tensor.matmul_mx(
+                    out=acc[:],
+                    lhsT=x_codes[:, g, 2 * P * m : 2 * P * (m + 1)].bitcast(FP4X4),
+                    lhsT_scale=x_planes[:, g, P * m : P * (m + 1)],
+                    rhs=w_codes[u][:, g, 2 * c0 : 2 * (c0 + cols)].bitcast(FP4X4),
+                    rhs_scale=w_planes[u][:, g, c0 : c0 + cols],
+                    start=(g == 0),
+                    stop=(g == PASSES - 1),
+                )
+            return acc
+
+        def products(acc, m, t1, t2):
+            pairs = acc[:].rearrange("p (h j e) -> p h j e", h=HEADS, e=2)
+            nc.vector.tensor_tensor(
+                    out=t1.rearrange("p (h j e) -> p h j e", h=HEADS, e=2),
+                    in0=cos_tab[:, m, :, :].unsqueeze(1).to_broadcast(by_head),
+                    in1=pairs,
+                    op=ALU.mult,
+            )
+            nc.vector.tensor_tensor(
+                    out=t2.rearrange("p (h j e) -> p h j e", h=HEADS, e=2),
+                    in0=sin_tab[:, m, :, :].unsqueeze(1).to_broadcast(by_head),
+                    in1=pairs[:, :, :, ::-1],
+                    op=ALU.mult,
             )
 
-        def rope(acc, n, m, index):
-            out_view, oc0 = blocks[n][2], blocks[n][3]
-            heads = BLOCK // HEAD
-            by_head = [P, heads, PAIRS, 2]
-            y = work.tile([P, BLOCK], F32, name="y")
-            t1 = work.tile([P, BLOCK], F32, name="t1")
-            t2 = work.tile([P, BLOCK], F32, name="t2")
-            pairs = acc[:].rearrange("p (h j e) -> p h j e", h=heads, e=2)
-            nc.vector.tensor_tensor(
-                out=t1[:].rearrange("p (h j e) -> p h j e", h=heads, e=2),
-                in0=pairs,
-                in1=cos_tab[:, m, :, :].unsqueeze(1).to_broadcast(by_head),
-                op=ALU.mult,
-            )
-            nc.vector.tensor_tensor(
-                out=t2[:].rearrange("p (h j e) -> p h j e", h=heads, e=2),
-                in0=pairs[:, :, :, ::-1],
-                in1=sin_tab[:, m, :, :].unsqueeze(1).to_broadcast(by_head),
-                op=ALU.mult,
-            )
-            if index % VECTOR_ADD_EVERY == VECTOR_ADD_EVERY - 1:
-                nc.vector.tensor_tensor(out=y[:], in0=t1[:], in1=t2[:], op=ALU.add)
-            else:
-                nc.gpsimd.tensor_tensor(out=y[:], in0=t1[:], in1=t2[:], op=ALU.add)
-            nc.sync.dma_start(out=out_view[P * m : P * (m + 1), oc0 : oc0 + BLOCK], in_=y[:])
+        pair_index = 0
+        for block in rope_blocks:
+            out_view, oc0 = block[2], block[3]
+            for m0 in (0, 2):
+                t1 = work.tile([P, 2, BLOCK], F32, name="t1")
+                t2 = work.tile([P, 2, BLOCK], F32, name="t2")
+                y = work.tile([P, 2, BLOCK], F32, name="y")
+                last = pair_index == 2 * len(rope_blocks) - 1
+                store = nc.scalar if pair_index < EARLY_STORES else nc.sync
+                for h in (0, 1):
+                    acc = group(block, m0 + h)
+                    products(acc, m0 + h, t1[:, h, :], t2[:, h, :])
+                    if last:
+                        adder = nc.gpsimd if h == 0 else nc.vector
+                        adder.tensor_tensor(out=y[:, h, :], in0=t1[:, h, :], in1=t2[:, h, :], op=ALU.add)
+                        m = m0 + h
+                        store.dma_start(out=out_view[P * m : P * (m + 1), oc0 : oc0 + BLOCK], in_=y[:, h, :])
+                if not last:
+                    nc.gpsimd.tensor_tensor(
+                        out=y[:].rearrange("p a c -> p (a c)"),
+                        in0=t1[:].rearrange("p a c -> p (a c)"),
+                        in1=t2[:].rearrange("p a c -> p (a c)"),
+                        op=ALU.add,
+                    )
+                    store.dma_start(
+                        out=out_view[P * m0 : P * (m0 + 2), oc0 : oc0 + BLOCK].rearrange("(a p) c -> p a c", p=P),
+                        in_=y[:],
+                    )
+                pair_index += 1
 
-        def plain(acc, n, m, first=0, cols=BLOCK):
-            out_view, oc0 = blocks[n][2], blocks[n][3] + first
+        def plain(m, first, cols):
+            acc = group(v_block, m, first, cols)
             v = work.tile([P, cols], F32, name="v", bufs=4)
             nc.scalar.copy(out=v[:], in_=acc[:])
-            nc.scalar.dma_start(out=out_view[P * m : P * (m + 1), oc0 : oc0 + cols], in_=v[:])
+            nc.scalar.dma_start(out=v_out[P * m : P * (m + 1), first : first + cols], in_=v[:])
 
-        groups = [(n, m) for n in range(len(blocks)) for m in range(TOKEN_TILES)]
-        index = 0
-        acc_a = psum.tile([P, BLOCK], F32, name="acc")
-        acc_b = psum.tile([P, BLOCK], F32, name="acc")
-        for g in range(PASSES):
-            one_pass(acc_a, 0, 0, g)
-            one_pass(acc_b, 0, 1, g)
-        rope(acc_a, 0, 0, 0)
-        rope(acc_b, 0, 1, 1)
-        index = 2
-        for n, m in groups[index:-1]:
-            acc = psum.tile([P, BLOCK], F32, name="acc")
-            for g in range(PASSES):
-                one_pass(acc, n, m, g)
-            if blocks[n][4]:
-                rope(acc, n, m, index)
-            else:
-                plain(acc, n, m)
-            index += 1
-        n, m = groups[-1]
-        half = BLOCK // 2
-        for first in (0, half):
-            acc = psum.tile([P, half], F32, name="acc")
-            for g in range(PASSES):
-                one_pass(acc, n, m, g, first, half)
-            plain(acc, n, m, first, half)
+        for m in range(TOKEN_TILES - 1):
+            plain(m, 0, BLOCK)
+        plain(TOKEN_TILES - 1, 0, BLOCK // 2)
+        plain(TOKEN_TILES - 1, BLOCK // 2, BLOCK // 2)

@@ -226,34 +226,41 @@ def tile_rptattention_pa_kernel(
                     op=ALU.mult,
             )
 
+        def add_and_store(adder, store, block, m, banks, t1, t2, y):
+            out_view, oc0 = block[2], block[3]
+            adder.tensor_tensor(
+                out=y.rearrange("p a c -> p (a c)"),
+                in0=t1.rearrange("p a c -> p (a c)"),
+                in1=t2.rearrange("p a c -> p (a c)"),
+                op=ALU.add,
+            )
+            store.dma_start(
+                out=out_view[P * m : P * (m + banks), oc0 : oc0 + BLOCK].rearrange("(a p) c -> p a c", p=P),
+                in_=y,
+            )
+
+        pair_count = 2 * len(rope_blocks)
         pair_index = 0
         for block in rope_blocks:
-            out_view, oc0 = block[2], block[3]
             for m0 in (0, 2):
                 t1 = work.tile([P, 2, BLOCK], F32, name="t1")
                 t2 = work.tile([P, 2, BLOCK], F32, name="t2")
                 y = work.tile([P, 2, BLOCK], F32, name="y")
-                last = pair_index == 2 * len(rope_blocks) - 1
                 store = nc.scalar if pair_index < EARLY_STORES else nc.sync
                 for h in (0, 1):
                     acc = group(block, m0 + h)
                     products(acc, m0 + h, t1[:, h, :], t2[:, h, :])
-                    if last:
-                        adder = nc.gpsimd if h == 0 else nc.vector
-                        adder.tensor_tensor(out=y[:, h, :], in0=t1[:, h, :], in1=t2[:, h, :], op=ALU.add)
-                        m = m0 + h
-                        store.dma_start(out=out_view[P * m : P * (m + 1), oc0 : oc0 + BLOCK], in_=y[:, h, :])
-                if not last:
-                    nc.gpsimd.tensor_tensor(
-                        out=y[:].rearrange("p a c -> p (a c)"),
-                        in0=t1[:].rearrange("p a c -> p (a c)"),
-                        in1=t2[:].rearrange("p a c -> p (a c)"),
-                        op=ALU.add,
-                    )
-                    store.dma_start(
-                        out=out_view[P * m0 : P * (m0 + 2), oc0 : oc0 + BLOCK].rearrange("(a p) c -> p a c", p=P),
-                        in_=y[:],
-                    )
+                    if pair_index == 0:
+                        add_and_store(
+                            nc.gpsimd, store, block, m0 + h, 1, t1[:, h : h + 1, :], t2[:, h : h + 1, :], y[:, h : h + 1, :]
+                        )
+                if pair_index == pair_count - 1:
+                    for h in (0, 1):
+                        add_and_store(
+                            nc.vector, store, block, m0 + h, 1, t1[:, h : h + 1, :], t2[:, h : h + 1, :], y[:, h : h + 1, :]
+                        )
+                elif pair_index > 0:
+                    add_and_store(nc.gpsimd, store, block, m0, 2, t1[:], t2[:], y[:])
                 pair_index += 1
 
         def plain(m, first, cols):

@@ -23,6 +23,7 @@ HEADS = BLOCK // HEAD
 ROPE_THETA = 10000.0
 TWO_PI = 2.0 * math.pi
 WARM_MATMULS = 12
+VECTOR_ADDS = 2
 EARLY_STORES = 5
 
 
@@ -87,18 +88,15 @@ def tile_rptattention_pa_kernel(
             w_codes.append(wc)
             w_planes.append(wp)
 
-        def load_scale_quadrant(planes, scales, c0, cols, q):
-            nc.sync.dma_start(
-                out=planes[32 * q : 32 * q + 4, :, :].bitcast(I32),
-                in_=scales[:, 4 * q : 4 * q + 4, c0 : c0 + cols].rearrange("g r n -> r g n").bitcast(I32),
-            )
+        def load_scales(planes, scales, c0, cols):
+            for q in range(4):
+                nc.sync.dma_start(
+                    out=planes[32 * q : 32 * q + 4, :, :].bitcast(I32),
+                    in_=scales[:, 4 * q : 4 * q + 4, c0 : c0 + cols].rearrange("g r n -> r g n").bitcast(I32),
+                )
 
-        def load_x_scales(q):
-            load_scale_quadrant(x_planes, hidden_states_scales, 0, BLOCK, q)
-
-        def load_unit_scales(u, quadrants=(0, 1, 2, 3)):
-            for q in quadrants:
-                load_scale_quadrant(w_planes[u], units[u][1], units[u][2], units[u][3], q)
+        def load_unit_scales(u):
+            load_scales(w_planes[u], units[u][1], units[u][2], units[u][3])
 
         def load_unit_codes(u):
             words, c0, cols = units[u][0], units[u][2], units[u][3]
@@ -106,6 +104,9 @@ def tile_rptattention_pa_kernel(
                 out=w_codes[u][:].bitcast(I32),
                 in_=words[:, :, 2 * c0 : 2 * (c0 + cols)].rearrange("g p c -> p g c").bitcast(I32),
             )
+
+        nc.vector.memset(x_planes[:].bitcast(I32), 0)
+        nc.vector.memset(w_planes[0][:].bitcast(I32), 0)
 
         def load_first_codes(g0, g1):
             nc.sync.dma_start(
@@ -117,11 +118,8 @@ def tile_rptattention_pa_kernel(
                 in_=wq_words[g0:g1, :, 0 : 2 * BLOCK].rearrange("g p c -> p g c").bitcast(I32),
             )
 
-        nc.vector.memset(x_planes[:].bitcast(I32), 0)
-        nc.vector.memset(w_planes[0][:].bitcast(I32), 0)
         load_first_codes(0, 1)
-        for q in range(4):
-            load_x_scales(q)
+        load_scales(x_planes, hidden_states_scales, 0, BLOCK)
         load_unit_scales(0)
         load_first_codes(1, PASSES)
 
@@ -136,9 +134,6 @@ def tile_rptattention_pa_kernel(
                 out=freq[:, s : 2 * s], in0=freq[:, 0:s], scalar1=ratio**s, scalar2=1.0, op0=ALU.mult, op1=ALU.mult
             )
             s *= 2
-        sign = keep.tile([P, PAIRS, 2], F32, name="sign")
-        nc.gpsimd.memset(sign[:], 1.0)
-        nc.gpsimd.memset(sign[:, :, 0:1], -1.0)
         for u in range(2, len(units)):
             nc.gpsimd.memset(w_planes[u][:].bitcast(F32), 0.0)
 
@@ -183,86 +178,77 @@ def tile_rptattention_pa_kernel(
 
         sin_cos = keep.tile([P, 2, TOKEN_TILES, PAIRS], F32, name="sin_cos")
         nc.scalar.activation(out=sin_cos[:], in_=neg_frac[:], func=ACTF.Sin, scale=-TWO_PI)
-        full = [P, TOKEN_TILES, PAIRS, 2]
-        cos_tab = keep.tile(full, F32, name="cos_tab")
-        sin_tab = keep.tile(full, F32, name="sin_tab")
-        nc.vector.tensor_copy(out=cos_tab[:], in_=sin_cos[:, 1, :, :].unsqueeze(3).to_broadcast(full))
-        nc.vector.tensor_tensor(
-            out=sin_tab[:],
-            in0=sin_cos[:, 0, :, :].unsqueeze(3).to_broadcast(full),
-            in1=sign[:].unsqueeze(1).to_broadcast(full),
-            op=ALU.mult,
+        table = keep.tile([P, TOKEN_TILES, 2, PAIRS, 2], F32, name="table")
+        nc.vector.tensor_copy(out=table[:, :, 0, :, 0], in_=sin_cos[:, 1, :, :])
+        nc.vector.tensor_copy(out=table[:, :, 0, :, 1], in_=sin_cos[:, 0, :, :])
+        nc.vector.tensor_scalar(
+            out=table[:, :, 1, :, 0], in0=sin_cos[:, 0, :, :], scalar1=-1.0, scalar2=None, op0=ALU.mult
         )
+        nc.vector.tensor_copy(out=table[:, :, 1, :, 1], in_=sin_cos[:, 1, :, :])
 
-        by_head = [P, HEADS, PAIRS, 2]
+        spread = [P, 2, HEADS, PAIRS, 2]
+
+        def one_pass(acc, block, m, g, first=0, cols=BLOCK):
+            u, c0 = block[0], block[1] + first
+            nc.tensor.matmul_mx(
+                out=acc[:],
+                lhsT=x_codes[:, g, 2 * P * m : 2 * P * (m + 1)].bitcast(FP4X4),
+                lhsT_scale=x_planes[:, g, P * m : P * (m + 1)],
+                rhs=w_codes[u][:, g, 2 * c0 : 2 * (c0 + cols)].bitcast(FP4X4),
+                rhs_scale=w_planes[u][:, g, c0 : c0 + cols],
+                start=(g == 0),
+                stop=(g == PASSES - 1),
+            )
 
         def group(block, m, first=0, cols=BLOCK):
-            u, c0 = block[0], block[1] + first
             acc = psum.tile([P, cols], F32, name="acc")
             for g in range(PASSES):
-                nc.tensor.matmul_mx(
-                    out=acc[:],
-                    lhsT=x_codes[:, g, 2 * P * m : 2 * P * (m + 1)].bitcast(FP4X4),
-                    lhsT_scale=x_planes[:, g, P * m : P * (m + 1)],
-                    rhs=w_codes[u][:, g, 2 * c0 : 2 * (c0 + cols)].bitcast(FP4X4),
-                    rhs_scale=w_planes[u][:, g, c0 : c0 + cols],
-                    start=(g == 0),
-                    stop=(g == PASSES - 1),
-                )
+                one_pass(acc, block, m, g, first, cols)
             return acc
 
-        def products(acc, m, t1, t2):
-            pairs = acc[:].rearrange("p (h j e) -> p h j e", h=HEADS, e=2)
+        def products(acc, m, ab):
             nc.vector.tensor_tensor(
-                    out=t1.rearrange("p (h j e) -> p h j e", h=HEADS, e=2),
-                    in0=cos_tab[:, m, :, :].unsqueeze(1).to_broadcast(by_head),
-                    in1=pairs,
-                    op=ALU.mult,
-            )
-            nc.vector.tensor_tensor(
-                    out=t2.rearrange("p (h j e) -> p h j e", h=HEADS, e=2),
-                    in0=sin_tab[:, m, :, :].unsqueeze(1).to_broadcast(by_head),
-                    in1=pairs[:, :, :, ::-1],
-                    op=ALU.mult,
+                out=ab.rearrange("p w (h j e) -> p w h j e", h=HEADS, e=2),
+                in0=table[:, m, :, :, :].unsqueeze(2).to_broadcast(spread),
+                in1=acc[:].rearrange("p (h j w) -> p w h j", h=HEADS, w=2).unsqueeze(4).to_broadcast(spread),
+                op=ALU.mult,
             )
 
-        def add_and_store(adder, store, block, m, banks, t1, t2, y):
+        def add_and_store(adder, store, block, m, banks, ab, y):
             out_view, oc0 = block[2], block[3]
-            adder.tensor_tensor(
-                out=y.rearrange("p a c -> p (a c)"),
-                in0=t1.rearrange("p a c -> p (a c)"),
-                in1=t2.rearrange("p a c -> p (a c)"),
-                op=ALU.add,
-            )
+            adder.tensor_tensor(out=y, in0=ab[:, :, 0, :], in1=ab[:, :, 1, :], op=ALU.add)
             store.dma_start(
                 out=out_view[P * m : P * (m + banks), oc0 : oc0 + BLOCK].rearrange("(a p) c -> p a c", p=P),
                 in_=y,
             )
 
-        pair_count = 2 * len(rope_blocks)
+        bank_count = TOKEN_TILES * len(rope_blocks)
+        left_to_vector = []
         pair_index = 0
         for block in rope_blocks:
             for m0 in (0, 2):
-                t1 = work.tile([P, 2, BLOCK], F32, name="t1")
-                t2 = work.tile([P, 2, BLOCK], F32, name="t2")
+                ab = work.tile([P, 2, 2, BLOCK], F32, name="ab")
                 y = work.tile([P, 2, BLOCK], F32, name="y")
                 store = nc.scalar if pair_index < EARLY_STORES else nc.sync
+                on_vector = [2 * pair_index + h >= bank_count - VECTOR_ADDS for h in (0, 1)]
+                single = pair_index == 0 or on_vector[0] or on_vector[1]
+                if pair_index == 0:
+                    accs = None
+                    order = (0, 1)
+                else:
+                    accs = [group(block, m0), group(block, m0 + 1)]
+                    order = (0, 1)
+                for h in order:
+                    acc = group(block, m0 + h) if accs is None else accs[h]
+                    products(acc, m0 + h, ab[:, h, :, :])
                 for h in (0, 1):
-                    acc = group(block, m0 + h)
-                    products(acc, m0 + h, t1[:, h, :], t2[:, h, :])
-                    if pair_index == 0:
-                        add_and_store(
-                            nc.gpsimd, store, block, m0 + h, 1, t1[:, h : h + 1, :], t2[:, h : h + 1, :], y[:, h : h + 1, :]
-                        )
-                if pair_index == pair_count - 1:
-                    for h in (0, 1):
-                        add_and_store(
-                            nc.vector, store, block, m0 + h, 1, t1[:, h : h + 1, :], t2[:, h : h + 1, :], y[:, h : h + 1, :]
-                        )
-                elif pair_index > 0:
-                    add_and_store(nc.gpsimd, store, block, m0, 2, t1[:], t2[:], y[:])
+                    if on_vector[h]:
+                        left_to_vector.append((store, block, m0 + h, ab[:, h : h + 1, :, :], y[:, h : h + 1, :]))
+                    elif single:
+                        add_and_store(nc.gpsimd, store, block, m0 + h, 1, ab[:, h : h + 1, :, :], y[:, h : h + 1, :])
+                if not single:
+                    add_and_store(nc.gpsimd, store, block, m0, 2, ab[:], y[:])
                 pair_index += 1
-
         def plain(m, first, cols):
             acc = group(v_block, m, first, cols)
             v = work.tile([P, cols], F32, name="v", bufs=4)
@@ -273,3 +259,5 @@ def tile_rptattention_pa_kernel(
             plain(m, 0, BLOCK)
         plain(TOKEN_TILES - 1, 0, BLOCK // 2)
         plain(TOKEN_TILES - 1, BLOCK // 2, BLOCK // 2)
+        for store, block, m, ab, y in left_to_vector:
+            add_and_store(nc.vector, store, block, m, 1, ab, y)

@@ -22,9 +22,10 @@ PAIRS = HEAD // 2
 HEADS = BLOCK // HEAD
 ROPE_THETA = 10000.0
 TWO_PI = 2.0 * math.pi
-WARM_MATMULS = 12
+WARM_MATMULS = 8
 VECTOR_ADDS = 2
 EARLY_STORES = 5
+PLANE_TILES = 3
 
 
 def tile_rptattention_pa_kernel(
@@ -46,33 +47,24 @@ def tile_rptattention_pa_kernel(
     k_out = out_1.rearrange("b s h d -> (b s) (h d)")
     v_out = out_2.rearrange("b s h d -> (b s) (h d)")
 
-    units = [
-        (wq_words, wq_scales, 0, BLOCK),
-        (wq_words, wq_scales, BLOCK, BLOCK),
-        (wq_words, wq_scales, 2 * BLOCK, 2 * BLOCK),
-        (wk_words, wk_scales, 0, BLOCK),
-        (wv_words, wv_scales, 0, BLOCK),
-    ]
-    rope_blocks = [
-        (0, 0, q_out, 0),
-        (1, 0, q_out, BLOCK),
-        (2, 0, q_out, 2 * BLOCK),
-        (2, BLOCK, q_out, 3 * BLOCK),
-        (3, 0, k_out, 0),
-    ]
-    v_block = (4, 0, v_out, 0)
+    blocks = [(wq_words, wq_scales, BLOCK * n, q_out, BLOCK * n) for n in range(4)]
+    blocks.append((wk_words, wk_scales, 0, k_out, 0))
+    blocks.append((wv_words, wv_scales, 0, v_out, 0))
+    rope_blocks = len(blocks) - 1
 
     with ExitStack() as ctx:
         keep = ctx.enter_context(tc.tile_pool(name="keep", bufs=1))
         work = ctx.enter_context(tc.tile_pool(name="work", bufs=5))
         psum = ctx.enter_context(tc.psum_pool(name="psum", bufs=8))
 
+        pos = keep.tile([P, TOKEN_TILES], F32, name="pos")
+        nc.gpsimd.iota(
+            out=pos[:], pattern=[[P, TOKEN_TILES]], base=0, channel_multiplier=1, allow_small_or_imprecise_dtypes=True
+        )
         warm_bf = keep.tile([P, P + BLOCK], BF16, name="warm_bf")
         nc.gpsimd.memset(warm_bf[:], 0.0)
-        warm_in = keep.tile([P, 1], F32, name="warm_in")
         warm_out = keep.tile([P, 1], F32, name="warm_out")
-        nc.gpsimd.memset(warm_in[:], 0.0)
-        nc.scalar.activation(out=warm_out[:], in_=warm_in[:], func=ACTF.Sin)
+        nc.scalar.activation(out=warm_out[:], in_=pos[:, 0:1], func=ACTF.Sin, scale=0.0)
         warm_acc = psum.tile([P, BLOCK], F32, name="acc")
         for i in range(WARM_MATMULS):
             nc.tensor.matmul(out=warm_acc[:], lhsT=warm_bf[:, 0:P], rhs=warm_bf[:, P : P + BLOCK], start=True, stop=True)
@@ -80,177 +72,186 @@ def tile_rptattention_pa_kernel(
         x_codes = keep.tile([P, PASSES, 2 * BLOCK], U8, name="x_codes", align_bytes=64)
         x_planes = keep.tile([P, PASSES, BLOCK], U8, name="x_planes", align_bytes=64)
         w_codes = []
-        w_planes = []
-        for u in range(len(units)):
-            cols = units[u][3]
-            wc = keep.tile([P, PASSES, 2 * cols], U8, name="w_codes%d" % u, align_bytes=64)
-            wp = keep.tile([P, PASSES, cols], U8, name="w_planes%d" % u, align_bytes=64)
+        for n in range(len(blocks)):
+            wc = keep.tile([P, PASSES, 2 * BLOCK], U8, name="w_codes%d" % n, align_bytes=64)
             w_codes.append(wc)
+        w_planes = []
+        for i in range(PLANE_TILES):
+            wp = keep.tile([P, PASSES, BLOCK], U8, name="w_planes%d" % i, align_bytes=64)
             w_planes.append(wp)
 
-        def load_scales(planes, scales, c0, cols):
+        def load_scales(planes, scales, c0):
             for q in range(4):
                 nc.sync.dma_start(
                     out=planes[32 * q : 32 * q + 4, :, :].bitcast(I32),
-                    in_=scales[:, 4 * q : 4 * q + 4, c0 : c0 + cols].rearrange("g r n -> r g n").bitcast(I32),
+                    in_=scales[:, 4 * q : 4 * q + 4, c0 : c0 + BLOCK].rearrange("g r n -> r g n").bitcast(I32),
                 )
 
-        def load_unit_scales(u):
-            load_scales(w_planes[u], units[u][1], units[u][2], units[u][3])
+        def load_block_scales(n):
+            load_scales(w_planes[n % PLANE_TILES], blocks[n][1], blocks[n][2])
 
-        def load_unit_codes(u):
-            words, c0, cols = units[u][0], units[u][2], units[u][3]
+        def load_block_codes(n):
+            words, c0 = blocks[n][0], blocks[n][2]
             nc.sync.dma_start(
-                out=w_codes[u][:].bitcast(I32),
-                in_=words[:, :, 2 * c0 : 2 * (c0 + cols)].rearrange("g p c -> p g c").bitcast(I32),
+                out=w_codes[n][:].bitcast(I32),
+                in_=words[:, :, 2 * c0 : 2 * (c0 + BLOCK)].rearrange("g p c -> p g c").bitcast(I32),
             )
 
         nc.vector.memset(x_planes[:].bitcast(I32), 0)
         nc.vector.memset(w_planes[0][:].bitcast(I32), 0)
 
-        def load_first_codes(g0, g1):
-            nc.sync.dma_start(
-                out=x_codes[:, g0:g1, :].bitcast(I32),
-                in_=hidden_states_words[g0:g1].rearrange("g p c -> p g c").bitcast(I32),
-            )
-            nc.sync.dma_start(
-                out=w_codes[0][:, g0:g1, :].bitcast(I32),
-                in_=wq_words[g0:g1, :, 0 : 2 * BLOCK].rearrange("g p c -> p g c").bitcast(I32),
-            )
+        def load_first_codes(g):
+            nc.sync.dma_start(out=x_codes[:, g, :].bitcast(I32), in_=hidden_states_words[g].bitcast(I32))
+            nc.sync.dma_start(out=w_codes[0][:, g, :].bitcast(I32), in_=wq_words[g][:, 0 : 2 * BLOCK].bitcast(I32))
 
-        load_first_codes(0, 1)
-        load_scales(x_planes, hidden_states_scales, 0, BLOCK)
-        load_unit_scales(0)
-        load_first_codes(1, PASSES)
+        load_first_codes(0)
+        load_scales(x_planes, hidden_states_scales, 0)
+        load_block_scales(0)
+        for g in range(1, PASSES):
+            load_first_codes(g)
+        load_block_codes(1)
 
-        pos_i = keep.tile([P, TOKEN_TILES], I32, name="pos_i")
-        nc.gpsimd.iota(out=pos_i[:], pattern=[[P, TOKEN_TILES]], base=0, channel_multiplier=1)
-        freq = keep.tile([P, PAIRS], F32, name="freq")
-        nc.gpsimd.memset(freq[:, 0:1], 1.0)
         ratio = ROPE_THETA ** (-2.0 / HEAD)
-        s = 1
-        while s < PAIRS:
-            nc.gpsimd.tensor_scalar(
-                out=freq[:, s : 2 * s], in0=freq[:, 0:s], scalar1=ratio**s, scalar2=1.0, op0=ALU.mult, op1=ALU.mult
-            )
-            s *= 2
-        for u in range(2, len(units)):
-            nc.gpsimd.memset(w_planes[u][:].bitcast(F32), 0.0)
-
-        pos_f = keep.tile([P, TOKEN_TILES], F32, name="pos_f")
-        nc.vector.tensor_copy(out=pos_f[:], in_=pos_i[:])
-        turns = keep.tile([P, 2, TOKEN_TILES, PAIRS], F32, name="turns")
-        for t in range(TOKEN_TILES):
+        ones = keep.tile([P, 4], F32, name="ones")
+        nc.vector.memset(ones[:], 1.0)
+        per_turn = keep.tile([P, PAIRS], F32, name="per_turn")
+        for i in range(4):
             nc.vector.tensor_scalar(
-                out=turns[:, 0, t, :],
-                in0=freq[:],
-                scalar1=pos_f[:, t : t + 1],
-                scalar2=1.0 / TWO_PI,
-                op0=ALU.mult,
-                op1=ALU.mult,
+                out=per_turn[:, i : i + 1], in0=ones[:, i : i + 1], scalar1=ratio**i / TWO_PI, scalar2=None, op0=ALU.mult
             )
-        nc.vector.tensor_scalar(
-            out=turns[:, 1, :, :], in0=turns[:, 0, :, :], scalar1=0.25, scalar2=None, op0=ALU.add
-        )
-        whole = keep.tile([P, 2, TOKEN_TILES, PAIRS], I32, name="whole")
-        nc.vector.tensor_copy(out=whole[:], in_=turns[:])
-        frac = keep.tile([P, 2, TOKEN_TILES, PAIRS], F32, name="frac")
-        nc.vector.tensor_tensor(out=frac[:], in0=turns[:], in1=whole[:], op=ALU.subtract)
-        neg_frac = keep.tile([P, 2, TOKEN_TILES, PAIRS], F32, name="neg_frac")
-        nc.vector.scalar_tensor_tensor(
-            out=neg_frac[:].rearrange("p a t j -> p (a t j)"),
-            in0=frac[:].rearrange("p a t j -> p (a t j)"),
-            scalar=0.5,
-            in1=frac[:].rearrange("p a t j -> p (a t j)"),
-            op0=ALU.is_gt,
-            op1=ALU.subtract,
-        )
-        nc.vector.memset(w_planes[1][:].bitcast(I32), 0)
+        for width in (4, 16):
+            for k in range(1, 4):
+                nc.vector.tensor_scalar(
+                    out=per_turn[:, k * width : (k + 1) * width],
+                    in0=per_turn[:, 0:width],
+                    scalar1=ratio ** (k * width),
+                    scalar2=None,
+                    op0=ALU.mult,
+                )
+        halves = (0, 1)
+        turns = []
+        whole = []
+        frac = []
+        for half in halves:
+            tu = keep.tile([P, 2, 2, PAIRS], F32, name="turns%d" % half)
+            wh = keep.tile([P, 2, 2, PAIRS], I32, name="whole%d" % half)
+            fr = keep.tile([P, 2, 2, PAIRS], F32, name="frac%d" % half)
+            turns.append(tu)
+            whole.append(wh)
+            frac.append(fr)
+        for t in range(TOKEN_TILES):
+            tu = turns[t // 2]
+            nc.vector.tensor_scalar(
+                out=tu[:, t % 2, 0, :], in0=per_turn[:], scalar1=pos[:, t : t + 1], scalar2=None, op0=ALU.mult
+            )
+            nc.vector.tensor_scalar(
+                out=tu[:, t % 2, 1, :], in0=per_turn[:], scalar1=pos[:, t : t + 1], scalar2=0.25, op0=ALU.mult, op1=ALU.add
+            )
+        for half in halves:
+            nc.vector.tensor_copy(out=whole[half][:], in_=turns[half][:])
+        for half in halves:
+            nc.vector.tensor_tensor(out=frac[half][:], in0=turns[half][:], in1=whole[half][:], op=ALU.subtract)
+        for i in range(1, PLANE_TILES):
+            nc.vector.memset(w_planes[i][:].bitcast(I32), 0)
+        cos_tab = []
+        sin_tab = []
+        for half in halves:
+            trig = keep.tile([P, 2, 3, PAIRS], F32, name="trig%d" % half)
+            nc.scalar.activation(out=trig[:, :, 1:3, :], in_=frac[half][:], func=ACTF.Sin, scale=TWO_PI)
+            nc.scalar.activation(out=trig[:, :, 0, :], in_=frac[half][:, :, 0, :], func=ACTF.Sin, scale=-TWO_PI)
+            ct = keep.tile([P, 2, PAIRS, 2], F32, name="cos_tab%d" % half)
+            st = keep.tile([P, 2, PAIRS, 2], F32, name="sin_tab%d" % half)
+            nc.vector.tensor_copy(out=ct[:], in_=trig[:, :, 2, :].unsqueeze(3).to_broadcast([P, 2, PAIRS, 2]))
+            nc.vector.tensor_copy(out=st[:], in_=trig[:, :, 0:2, :].rearrange("p t k j -> p t j k"))
+            cos_tab.append(ct)
+            sin_tab.append(st)
 
-        load_unit_scales(1)
-        load_unit_codes(1)
-        load_unit_scales(2)
-        load_unit_codes(2)
-        load_unit_scales(3)
-        load_unit_scales(4)
-        load_unit_codes(3)
-        load_unit_codes(4)
+        load_block_scales(1)
+        load_block_scales(2)
+        for n in range(2, len(blocks)):
+            load_block_codes(n)
 
-        sin_cos = keep.tile([P, 2, TOKEN_TILES, PAIRS], F32, name="sin_cos")
-        nc.scalar.activation(out=sin_cos[:], in_=neg_frac[:], func=ACTF.Sin, scale=-TWO_PI)
-        table = keep.tile([P, TOKEN_TILES, 2, PAIRS, 2], F32, name="table")
-        nc.vector.tensor_copy(out=table[:, :, 0, :, 0], in_=sin_cos[:, 1, :, :])
-        nc.vector.tensor_copy(out=table[:, :, 0, :, 1], in_=sin_cos[:, 0, :, :])
-        nc.vector.tensor_scalar(
-            out=table[:, :, 1, :, 0], in0=sin_cos[:, 0, :, :], scalar1=-1.0, scalar2=None, op0=ALU.mult
-        )
-        nc.vector.tensor_copy(out=table[:, :, 1, :, 1], in_=sin_cos[:, 1, :, :])
+        by_head = [P, HEADS, PAIRS, 2]
 
-        spread = [P, 2, HEADS, PAIRS, 2]
-
-        def one_pass(acc, block, m, g, first=0, cols=BLOCK):
-            u, c0 = block[0], block[1] + first
+        def one_pass(acc, n, m, g, first=0, cols=BLOCK):
             nc.tensor.matmul_mx(
                 out=acc[:],
                 lhsT=x_codes[:, g, 2 * P * m : 2 * P * (m + 1)].bitcast(FP4X4),
                 lhsT_scale=x_planes[:, g, P * m : P * (m + 1)],
-                rhs=w_codes[u][:, g, 2 * c0 : 2 * (c0 + cols)].bitcast(FP4X4),
-                rhs_scale=w_planes[u][:, g, c0 : c0 + cols],
+                rhs=w_codes[n][:, g, 2 * first : 2 * (first + cols)].bitcast(FP4X4),
+                rhs_scale=w_planes[n % PLANE_TILES][:, g, first : first + cols],
                 start=(g == 0),
                 stop=(g == PASSES - 1),
             )
 
-        def group(block, m, first=0, cols=BLOCK):
+        def group(n, m, first=0, cols=BLOCK):
             acc = psum.tile([P, cols], F32, name="acc")
             for g in range(PASSES):
-                one_pass(acc, block, m, g, first, cols)
+                one_pass(acc, n, m, g, first, cols)
             return acc
 
-        def products(acc, m, ab):
+        def products(acc, m, t1, t2):
+            pairs = acc[:].rearrange("p (h j e) -> p h j e", h=HEADS, e=2)
             nc.vector.tensor_tensor(
-                out=ab.rearrange("p w (h j e) -> p w h j e", h=HEADS, e=2),
-                in0=table[:, m, :, :, :].unsqueeze(2).to_broadcast(spread),
-                in1=acc[:].rearrange("p (h j w) -> p w h j", h=HEADS, w=2).unsqueeze(4).to_broadcast(spread),
+                out=t1.rearrange("p (h j e) -> p h j e", h=HEADS, e=2),
+                in0=cos_tab[m // 2][:, m % 2, :, :].unsqueeze(1).to_broadcast(by_head),
+                in1=pairs,
+                op=ALU.mult,
+            )
+            nc.vector.tensor_tensor(
+                out=t2.rearrange("p (h j e) -> p h j e", h=HEADS, e=2),
+                in0=sin_tab[m // 2][:, m % 2, :, :].unsqueeze(1).to_broadcast(by_head),
+                in1=pairs[:, :, :, ::-1],
                 op=ALU.mult,
             )
 
-        def add_and_store(adder, store, block, m, banks, ab, y):
-            out_view, oc0 = block[2], block[3]
-            adder.tensor_tensor(out=y, in0=ab[:, :, 0, :], in1=ab[:, :, 1, :], op=ALU.add)
+        def add_and_store(adder, store, n, m, banks, t1, t2, y):
+            out_view, oc0 = blocks[n][3], blocks[n][4]
+            adder.tensor_tensor(
+                out=y.rearrange("p a c -> p (a c)"),
+                in0=t1.rearrange("p a c -> p (a c)"),
+                in1=t2.rearrange("p a c -> p (a c)"),
+                op=ALU.add,
+            )
             store.dma_start(
                 out=out_view[P * m : P * (m + banks), oc0 : oc0 + BLOCK].rearrange("(a p) c -> p a c", p=P),
                 in_=y,
             )
 
-        bank_count = TOKEN_TILES * len(rope_blocks)
+        head_a = psum.tile([P, BLOCK], F32, name="acc")
+        head_b = psum.tile([P, BLOCK], F32, name="acc")
+        for g in range(PASSES):
+            one_pass(head_a, 0, 0, g)
+            one_pass(head_b, 0, 1, g)
+        head_accs = [head_a, head_b]
+
+        bank_count = TOKEN_TILES * rope_blocks
         left_to_vector = []
         pair_index = 0
-        for block in rope_blocks:
+        for n in range(rope_blocks):
             for m0 in (0, 2):
-                ab = work.tile([P, 2, 2, BLOCK], F32, name="ab")
+                t1 = work.tile([P, 2, BLOCK], F32, name="t1")
+                t2 = work.tile([P, 2, BLOCK], F32, name="t2")
                 y = work.tile([P, 2, BLOCK], F32, name="y")
                 store = nc.scalar if pair_index < EARLY_STORES else nc.sync
                 on_vector = [2 * pair_index + h >= bank_count - VECTOR_ADDS for h in (0, 1)]
                 single = pair_index == 0 or on_vector[0] or on_vector[1]
-                if pair_index == 0:
-                    accs = None
-                    order = (0, 1)
-                else:
-                    accs = [group(block, m0), group(block, m0 + 1)]
-                    order = (0, 1)
-                for h in order:
-                    acc = group(block, m0 + h) if accs is None else accs[h]
-                    products(acc, m0 + h, ab[:, h, :, :])
                 for h in (0, 1):
+                    acc = head_accs[h] if pair_index == 0 else group(n, m0 + h)
+                    products(acc, m0 + h, t1[:, h, :], t2[:, h, :])
+                    one = (store, n, m0 + h, 1, t1[:, h : h + 1, :], t2[:, h : h + 1, :], y[:, h : h + 1, :])
                     if on_vector[h]:
-                        left_to_vector.append((store, block, m0 + h, ab[:, h : h + 1, :, :], y[:, h : h + 1, :]))
+                        left_to_vector.append(one)
                     elif single:
-                        add_and_store(nc.gpsimd, store, block, m0 + h, 1, ab[:, h : h + 1, :, :], y[:, h : h + 1, :])
+                        add_and_store(nc.gpsimd, *one)
                 if not single:
-                    add_and_store(nc.gpsimd, store, block, m0, 2, ab[:], y[:])
+                    add_and_store(nc.gpsimd, store, n, m0, 2, t1[:], t2[:], y[:])
                 pair_index += 1
+            if n + PLANE_TILES < len(blocks):
+                load_block_scales(n + PLANE_TILES)
+
         def plain(m, first, cols):
-            acc = group(v_block, m, first, cols)
+            acc = group(rope_blocks, m, first, cols)
             v = work.tile([P, cols], F32, name="v", bufs=4)
             nc.scalar.copy(out=v[:], in_=acc[:])
             nc.scalar.dma_start(out=v_out[P * m : P * (m + 1), first : first + cols], in_=v[:])
@@ -259,5 +260,5 @@ def tile_rptattention_pa_kernel(
             plain(m, 0, BLOCK)
         plain(TOKEN_TILES - 1, 0, BLOCK // 2)
         plain(TOKEN_TILES - 1, BLOCK // 2, BLOCK // 2)
-        for store, block, m, ab, y in left_to_vector:
-            add_and_store(nc.vector, store, block, m, 1, ab, y)
+        for one in left_to_vector:
+            add_and_store(nc.vector, *one)

@@ -23,7 +23,7 @@ HEADS = BLOCK // HEAD
 ROPE_THETA = 10000.0
 TWO_PI = 2.0 * math.pi
 WARM_MATMULS = 8
-VECTOR_ADDS = 2
+VECTOR_ADDS = 4
 EARLY_STORES = 5
 PLANE_TILES = 3
 

@@ -25,7 +25,8 @@ TWO_PI = 2.0 * math.pi
 WARM_MATMULS = 8
 VECTOR_ADDS = 4
 EARLY_STORES = 5
-PLANE_TILES = 3
+PLANE_TILES = 6
+EARLY_PLANES = 3
 
 
 def tile_rptattention_pa_kernel(
@@ -151,7 +152,7 @@ def tile_rptattention_pa_kernel(
             nc.vector.tensor_copy(out=whole[half][:], in_=turns[half][:])
         for half in halves:
             nc.vector.tensor_tensor(out=frac[half][:], in0=turns[half][:], in1=whole[half][:], op=ALU.subtract)
-        for i in range(1, PLANE_TILES):
+        for i in range(1, EARLY_PLANES):
             nc.vector.memset(w_planes[i][:].bitcast(I32), 0)
         cos_tab = []
         sin_tab = []
@@ -166,9 +167,14 @@ def tile_rptattention_pa_kernel(
             cos_tab.append(ct)
             sin_tab.append(st)
 
+        for i in range(EARLY_PLANES, PLANE_TILES):
+            nc.vector.memset(w_planes[i][:].bitcast(I32), 0)
+
         load_block_scales(1)
         load_block_scales(2)
-        for n in range(2, len(blocks)):
+        load_block_codes(2)
+        for n in range(3, len(blocks)):
+            load_block_scales(n)
             load_block_codes(n)
 
         by_head = [P, HEADS, PAIRS, 2]
@@ -252,7 +258,7 @@ def tile_rptattention_pa_kernel(
 
         def plain(m, first, cols):
             acc = group(rope_blocks, m, first, cols)
-            v = work.tile([P, cols], F32, name="v", bufs=4)
+            v = work.tile([P, cols], F32, name="v", bufs=5)
             nc.scalar.copy(out=v[:], in_=acc[:])
             nc.scalar.dma_start(out=v_out[P * m : P * (m + 1), first : first + cols], in_=v[:])
 

@@ -23,10 +23,14 @@ HEADS = BLOCK // HEAD
 ROPE_THETA = 10000.0
 TWO_PI = 2.0 * math.pi
 WARM_MATMULS = 8
-VECTOR_ADDS = 4
+VECTOR_ADDS = 1
 EARLY_STORES = 5
 PLANE_TILES = 6
-EARLY_PLANES = 3
+LOAD_ORDER = (1, 5, 2, 3, 4)
+EARLY_PLANES = 2
+VALUE_AFTER = (1, 3)
+LAST_CUT = (256, 128, 128)
+VALUE_PIECES = 3 + len(LAST_CUT)
 
 
 def tile_rptattention_pa_kernel(
@@ -152,8 +156,8 @@ def tile_rptattention_pa_kernel(
             nc.vector.tensor_copy(out=whole[half][:], in_=turns[half][:])
         for half in halves:
             nc.vector.tensor_tensor(out=frac[half][:], in0=turns[half][:], in1=whole[half][:], op=ALU.subtract)
-        for i in range(1, EARLY_PLANES):
-            nc.vector.memset(w_planes[i][:].bitcast(I32), 0)
+        for n in LOAD_ORDER[:EARLY_PLANES]:
+            nc.vector.memset(w_planes[n][:].bitcast(I32), 0)
         cos_tab = []
         sin_tab = []
         for half in halves:
@@ -167,13 +171,11 @@ def tile_rptattention_pa_kernel(
             cos_tab.append(ct)
             sin_tab.append(st)
 
-        for i in range(EARLY_PLANES, PLANE_TILES):
-            nc.vector.memset(w_planes[i][:].bitcast(I32), 0)
+        for n in LOAD_ORDER[EARLY_PLANES:]:
+            nc.vector.memset(w_planes[n][:].bitcast(I32), 0)
 
-        load_block_scales(1)
-        load_block_scales(2)
-        load_block_codes(2)
-        for n in range(3, len(blocks)):
+        load_block_scales(LOAD_ORDER[0])
+        for n in LOAD_ORDER[1:]:
             load_block_scales(n)
             load_block_codes(n)
 
@@ -231,7 +233,14 @@ def tile_rptattention_pa_kernel(
             one_pass(head_b, 0, 1, g)
         head_accs = [head_a, head_b]
 
+        def plain(m, first, cols):
+            acc = group(rope_blocks, m, first, cols)
+            v = work.tile([P, cols], F32, name="v", bufs=VALUE_PIECES)
+            nc.scalar.copy(out=v[:], in_=acc[:])
+            nc.scalar.dma_start(out=v_out[P * m : P * (m + 1), first : first + cols], in_=v[:])
+
         bank_count = TOKEN_TILES * rope_blocks
+        pair_count = bank_count // 2
         left_to_vector = []
         pair_index = 0
         for n in range(rope_blocks):
@@ -241,7 +250,7 @@ def tile_rptattention_pa_kernel(
                 y = work.tile([P, 2, BLOCK], F32, name="y")
                 store = nc.scalar if pair_index < EARLY_STORES else nc.sync
                 on_vector = [2 * pair_index + h >= bank_count - VECTOR_ADDS for h in (0, 1)]
-                single = pair_index == 0 or on_vector[0] or on_vector[1]
+                single = pair_index == 0 or pair_index >= pair_count - 2
                 for h in (0, 1):
                     acc = head_accs[h] if pair_index == 0 else group(n, m0 + h)
                     products(acc, m0 + h, t1[:, h, :], t2[:, h, :])
@@ -253,18 +262,13 @@ def tile_rptattention_pa_kernel(
                 if not single:
                     add_and_store(nc.gpsimd, store, n, m0, 2, t1[:], t2[:], y[:])
                 pair_index += 1
-            if n + PLANE_TILES < len(blocks):
-                load_block_scales(n + PLANE_TILES)
+            if n in VALUE_AFTER:
+                plain(VALUE_AFTER.index(n), 0, BLOCK)
 
-        def plain(m, first, cols):
-            acc = group(rope_blocks, m, first, cols)
-            v = work.tile([P, cols], F32, name="v", bufs=5)
-            nc.scalar.copy(out=v[:], in_=acc[:])
-            nc.scalar.dma_start(out=v_out[P * m : P * (m + 1), first : first + cols], in_=v[:])
-
-        for m in range(TOKEN_TILES - 1):
-            plain(m, 0, BLOCK)
-        plain(TOKEN_TILES - 1, 0, BLOCK // 2)
-        plain(TOKEN_TILES - 1, BLOCK // 2, BLOCK // 2)
+        plain(TOKEN_TILES - 2, 0, BLOCK)
+        first = 0
+        for cols in LAST_CUT:
+            plain(TOKEN_TILES - 1, first, cols)
+            first += cols
         for one in left_to_vector:
             add_and_store(nc.vector, *one)

@@ -23,10 +23,12 @@ HEADS = BLOCK // HEAD
 ROPE_THETA = 10000.0
 TWO_PI = 2.0 * math.pi
 WARM_MATMULS = 8
-VECTOR_ADDS = 1
-EARLY_STORES = 5
+VECTOR_ADDS = 3
+EARLY_STORES = 0
 PLANE_TILES = 6
 LOAD_ORDER = (1, 5, 2, 3, 4)
+FRONT_LOADS = 3
+LOAD_AFTER_PAIR = {0: 3, 2: 4}
 EARLY_PLANES = 2
 VALUE_AFTER = (1, 3)
 LAST_CUT = (256, 128, 128)
@@ -59,8 +61,9 @@ def tile_rptattention_pa_kernel(
 
     with ExitStack() as ctx:
         keep = ctx.enter_context(tc.tile_pool(name="keep", bufs=1))
-        work = ctx.enter_context(tc.tile_pool(name="work", bufs=5))
+        work = ctx.enter_context(tc.tile_pool(name="work", bufs=6))
         psum = ctx.enter_context(tc.psum_pool(name="psum", bufs=8))
+        ctx.enter_context(tc.manual_schedule(engines={mybir.EngineType.SP}))
 
         pos = keep.tile([P, TOKEN_TILES], F32, name="pos")
         nc.gpsimd.iota(
@@ -175,7 +178,7 @@ def tile_rptattention_pa_kernel(
             nc.vector.memset(w_planes[n][:].bitcast(I32), 0)
 
         load_block_scales(LOAD_ORDER[0])
-        for n in LOAD_ORDER[1:]:
+        for n in LOAD_ORDER[1:FRONT_LOADS]:
             load_block_scales(n)
             load_block_codes(n)
 
@@ -261,6 +264,9 @@ def tile_rptattention_pa_kernel(
                         add_and_store(nc.gpsimd, *one)
                 if not single:
                     add_and_store(nc.gpsimd, store, n, m0, 2, t1[:], t2[:], y[:])
+                if pair_index in LOAD_AFTER_PAIR:
+                    load_block_scales(LOAD_AFTER_PAIR[pair_index])
+                    load_block_codes(LOAD_AFTER_PAIR[pair_index])
                 pair_index += 1
             if n in VALUE_AFTER:
                 plain(VALUE_AFTER.index(n), 0, BLOCK)

@@ -77,15 +77,15 @@ def tile_rptattention_pa_kernel(
         for i in range(WARM_MATMULS):
             nc.tensor.matmul(out=warm_acc[:], lhsT=warm_bf[:, 0:P], rhs=warm_bf[:, P : P + BLOCK], start=True, stop=True)
 
-        x_codes = keep.tile([P, PASSES, 2 * BLOCK], U8, name="x_codes", align_bytes=64)
-        x_planes = keep.tile([P, PASSES, BLOCK], U8, name="x_planes", align_bytes=64)
+        x_codes = keep.tile([P, PASSES, 2 * BLOCK], U8, name="x_codes", align_bytes=256)
+        x_planes = keep.tile([P, PASSES, BLOCK], U8, name="x_planes", align_bytes=256)
         w_codes = []
         for n in range(len(blocks)):
-            wc = keep.tile([P, PASSES, 2 * BLOCK], U8, name="w_codes%d" % n, align_bytes=64)
+            wc = keep.tile([P, PASSES, 2 * BLOCK], U8, name="w_codes%d" % n, align_bytes=256)
             w_codes.append(wc)
         w_planes = []
         for i in range(PLANE_TILES):
-            wp = keep.tile([P, PASSES, BLOCK], U8, name="w_planes%d" % i, align_bytes=64)
+            wp = keep.tile([P, PASSES, BLOCK], U8, name="w_planes%d" % i, align_bytes=256)
             w_planes.append(wp)
 
         def load_scales(planes, scales, c0):

@@ -30,7 +30,7 @@ LOAD_ORDER = (1, 5, 2, 3, 4)
 FRONT_LOADS = 3
 LOAD_AFTER_PAIR = {0: 3, 2: 4}
 EARLY_PLANES = 2
-VALUE_AFTER = (1, 3)
+VALUE_AFTER = (2,)
 LAST_CUT = (256, 128, 128)
 VALUE_PIECES = 3 + len(LAST_CUT)
 
@@ -77,7 +77,10 @@ def tile_rptattention_pa_kernel(
         for i in range(WARM_MATMULS):
             nc.tensor.matmul(out=warm_acc[:], lhsT=warm_bf[:, 0:P], rhs=warm_bf[:, P : P + BLOCK], start=True, stop=True)
 
-        x_codes = keep.tile([P, PASSES, 2 * BLOCK], U8, name="x_codes", align_bytes=256)
+        x_codes = []
+        for i in range(2):
+            xc = keep.tile([P, PASSES, BLOCK], U8, name="x_codes%d" % i, align_bytes=256)
+            x_codes.append(xc)
         x_planes = keep.tile([P, PASSES, BLOCK], U8, name="x_planes", align_bytes=256)
         w_codes = []
         for n in range(len(blocks)):
@@ -108,15 +111,23 @@ def tile_rptattention_pa_kernel(
         nc.vector.memset(x_planes[:].bitcast(I32), 0)
         nc.vector.memset(w_planes[0][:].bitcast(I32), 0)
 
-        def load_first_codes(g):
-            nc.sync.dma_start(out=x_codes[:, g, :].bitcast(I32), in_=hidden_states_words[g].bitcast(I32))
+        def load_x_codes(i, g0, g1):
+            nc.sync.dma_start(
+                out=x_codes[i][:, g0:g1, :].bitcast(I32),
+                in_=hidden_states_words[g0:g1, :, BLOCK * i : BLOCK * (i + 1)].rearrange("g p c -> p g c").bitcast(I32),
+            )
+
+        def load_first_weights(g):
             nc.sync.dma_start(out=w_codes[0][:, g, :].bitcast(I32), in_=wq_words[g][:, 0 : 2 * BLOCK].bitcast(I32))
 
-        load_first_codes(0)
+        load_x_codes(0, 0, 1)
+        load_first_weights(0)
         load_scales(x_planes, hidden_states_scales, 0)
         load_block_scales(0)
+        load_x_codes(0, 1, PASSES)
         for g in range(1, PASSES):
-            load_first_codes(g)
+            load_first_weights(g)
+        load_x_codes(1, 0, PASSES)
         load_block_codes(1)
 
         ratio = ROPE_THETA ** (-2.0 / HEAD)
@@ -187,7 +198,7 @@ def tile_rptattention_pa_kernel(
         def one_pass(acc, n, m, g, first=0, cols=BLOCK):
             nc.tensor.matmul_mx(
                 out=acc[:],
-                lhsT=x_codes[:, g, 2 * P * m : 2 * P * (m + 1)].bitcast(FP4X4),
+                lhsT=x_codes[m // 2][:, g, 2 * P * (m % 2) : 2 * P * (m % 2 + 1)].bitcast(FP4X4),
                 lhsT_scale=x_planes[:, g, P * m : P * (m + 1)],
                 rhs=w_codes[n][:, g, 2 * first : 2 * (first + cols)].bitcast(FP4X4),
                 rhs_scale=w_planes[n % PLANE_TILES][:, g, first : first + cols],
@@ -231,8 +242,11 @@ def tile_rptattention_pa_kernel(
 
         head_a = psum.tile([P, BLOCK], F32, name="acc")
         head_b = psum.tile([P, BLOCK], F32, name="acc")
-        for g in range(PASSES):
+        one_pass(head_a, 0, 0, 0)
+        one_pass(head_b, 0, 1, 0)
+        for g in range(1, PASSES):
             one_pass(head_a, 0, 0, g)
+        for g in range(1, PASSES):
             one_pass(head_b, 0, 1, g)
         head_accs = [head_a, head_b]
 
@@ -271,7 +285,8 @@ def tile_rptattention_pa_kernel(
             if n in VALUE_AFTER:
                 plain(VALUE_AFTER.index(n), 0, BLOCK)
 
-        plain(TOKEN_TILES - 2, 0, BLOCK)
+        for m in range(len(VALUE_AFTER), TOKEN_TILES - 1):
+            plain(m, 0, BLOCK)
         first = 0
         for cols in LAST_CUT:
             plain(TOKEN_TILES - 1, first, cols)

@@ -23,14 +23,15 @@ HEADS = BLOCK // HEAD
 ROPE_THETA = 10000.0
 TWO_PI = 2.0 * math.pi
 WARM_MATMULS = 8
-VECTOR_ADDS = 3
+VECTOR_ADDS = 2
+REDUCE_PAIR = 7
 EARLY_STORES = 0
 PLANE_TILES = 6
 LOAD_ORDER = (1, 5, 2, 3, 4)
 FRONT_LOADS = 3
 LOAD_AFTER_PAIR = {0: 3, 2: 4}
 EARLY_PLANES = 2
-VALUE_AFTER = (2,)
+VALUE_AFTER = (3,)
 LAST_CUT = (256, 128, 128)
 VALUE_PIECES = 3 + len(LAST_CUT)
 
@@ -268,6 +269,18 @@ def tile_rptattention_pa_kernel(
                 store = nc.scalar if pair_index < EARLY_STORES else nc.sync
                 on_vector = [2 * pair_index + h >= bank_count - VECTOR_ADDS for h in (0, 1)]
                 single = pair_index == 0 or pair_index >= pair_count - 2
+                if pair_index == REDUCE_PAIR:
+                    both = (t1, t2)
+                    for h in (0, 1):
+                        acc = group(n, m0 + h)
+                        products(acc, m0 + h, both[h][:, 0, :], both[h][:, 1, :])
+                    nc.vector.tensor_reduce(
+                        out=y[:, 0, :], in_=t1[:].rearrange("p k c -> p c k"), axis=mybir.AxisListType.X, op=ALU.add
+                    )
+                    store.dma_start(out=blocks[n][3][P * m0 : P * (m0 + 1), blocks[n][4] : blocks[n][4] + BLOCK], in_=y[:, 0, :])
+                    add_and_store(nc.gpsimd, store, n, m0 + 1, 1, t2[:, 0:1, :], t2[:, 1:2, :], y[:, 1:2, :])
+                    pair_index += 1
+                    continue
                 for h in (0, 1):
                     acc = head_accs[h] if pair_index == 0 else group(n, m0 + h)
                     products(acc, m0 + h, t1[:, h, :], t2[:, h, :])

@@ -24,14 +24,15 @@ ROPE_THETA = 10000.0
 TWO_PI = 2.0 * math.pi
 WARM_MATMULS = 8
 VECTOR_ADDS = 2
-REDUCE_PAIR = 7
+REDUCE_PAIR = 8
 EARLY_STORES = 0
 PLANE_TILES = 6
 LOAD_ORDER = (1, 5, 2, 3, 4)
 FRONT_LOADS = 3
 LOAD_AFTER_PAIR = {0: 3, 2: 4}
 EARLY_PLANES = 2
-VALUE_AFTER = (3,)
+VALUE_AFTER = ()
+MID_VALUE_TILES = 1
 LAST_CUT = (256, 128, 128)
 VALUE_PIECES = 3 + len(LAST_CUT)
 
@@ -279,6 +280,7 @@ def tile_rptattention_pa_kernel(
                     )
                     store.dma_start(out=blocks[n][3][P * m0 : P * (m0 + 1), blocks[n][4] : blocks[n][4] + BLOCK], in_=y[:, 0, :])
                     add_and_store(nc.gpsimd, store, n, m0 + 1, 1, t2[:, 0:1, :], t2[:, 1:2, :], y[:, 1:2, :])
+                    plain(0, 0, BLOCK)
                     pair_index += 1
                     continue
                 for h in (0, 1):
@@ -298,7 +300,7 @@ def tile_rptattention_pa_kernel(
             if n in VALUE_AFTER:
                 plain(VALUE_AFTER.index(n), 0, BLOCK)
 
-        for m in range(len(VALUE_AFTER), TOKEN_TILES - 1):
+        for m in range(MID_VALUE_TILES, TOKEN_TILES - 1):
             plain(m, 0, BLOCK)
         first = 0
         for cols in LAST_CUT:

import math
from contextlib import ExitStack

import concourse.mybir as mybir

FLOPS = 2 * 512 * 2048 * 3072

F32 = mybir.dt.float32
BF16 = mybir.dt.bfloat16
I32 = mybir.dt.int32
U8 = mybir.dt.uint8
FP4X4 = mybir.dt.float4_e2m1fn_x4
ALU = mybir.AluOpType
ACTF = mybir.ActivationFunctionType

P = 128
PASSES = 4
TOKEN_TILES = 4
BLOCK = 512
HEAD = 128
PAIRS = HEAD // 2
HEADS = BLOCK // HEAD
ROPE_THETA = 10000.0
TWO_PI = 2.0 * math.pi
WARM_MATMULS = 8
VECTOR_ADDS = 2
REDUCE_PAIR = 8
EARLY_STORES = 0
PLANE_TILES = 6
LOAD_ORDER = (1, 5, 2, 3, 4)
FRONT_LOADS = 3
LOAD_AFTER_PAIR = {0: 3, 2: 4}
EARLY_PLANES = 2
VALUE_AFTER = ()
MID_VALUE_TILES = 1
LAST_CUT = (256, 128, 128)
VALUE_PIECES = 3 + len(LAST_CUT)


def tile_rptattention_pa_kernel(
    tc,
    hidden_states_words,
    hidden_states_scales,
    wq_words,
    wq_scales,
    wk_words,
    wk_scales,
    wv_words,
    wv_scales,
    out_0,
    out_1,
    out_2,
):
    nc = tc.nc
    q_out = out_0.rearrange("b s h d -> (b s) (h d)")
    k_out = out_1.rearrange("b s h d -> (b s) (h d)")
    v_out = out_2.rearrange("b s h d -> (b s) (h d)")

    blocks = [(wq_words, wq_scales, BLOCK * n, q_out, BLOCK * n) for n in range(4)]
    blocks.append((wk_words, wk_scales, 0, k_out, 0))
    blocks.append((wv_words, wv_scales, 0, v_out, 0))
    rope_blocks = len(blocks) - 1

    with ExitStack() as ctx:
        keep = ctx.enter_context(tc.tile_pool(name="keep", bufs=1))
        work = ctx.enter_context(tc.tile_pool(name="work", bufs=6))
        psum = ctx.enter_context(tc.psum_pool(name="psum", bufs=8))
        ctx.enter_context(tc.manual_schedule(engines={mybir.EngineType.SP}))

        pos = keep.tile([P, TOKEN_TILES], F32, name="pos")
        nc.gpsimd.iota(
            out=pos[:], pattern=[[P, TOKEN_TILES]], base=0, channel_multiplier=1, allow_small_or_imprecise_dtypes=True
        )
        warm_bf = keep.tile([P, P + BLOCK], BF16, name="warm_bf")
        nc.gpsimd.memset(warm_bf[:], 0.0)
        warm_out = keep.tile([P, 1], F32, name="warm_out")
        nc.scalar.activation(out=warm_out[:], in_=pos[:, 0:1], func=ACTF.Sin, scale=0.0)
        warm_acc = psum.tile([P, BLOCK], F32, name="acc")
        for i in range(WARM_MATMULS):
            nc.tensor.matmul(out=warm_acc[:], lhsT=warm_bf[:, 0:P], rhs=warm_bf[:, P : P + BLOCK], start=True, stop=True)

        x_codes = []
        for i in range(2):
            xc = keep.tile([P, PASSES, BLOCK], U8, name="x_codes%d" % i, align_bytes=256)
            x_codes.append(xc)
        x_planes = keep.tile([P, PASSES, BLOCK], U8, name="x_planes", align_bytes=256)
        w_codes = []
        for n in range(len(blocks)):
            wc = keep.tile([P, PASSES, 2 * BLOCK], U8, name="w_codes%d" % n, align_bytes=256)
            w_codes.append(wc)
        w_planes = []
        for i in range(PLANE_TILES):
            wp = keep.tile([P, PASSES, BLOCK], U8, name="w_planes%d" % i, align_bytes=256)
            w_planes.append(wp)

        def load_scales(planes, scales, c0):
            for q in range(4):
                nc.sync.dma_start(
                    out=planes[32 * q : 32 * q + 4, :, :].bitcast(I32),
                    in_=scales[:, 4 * q : 4 * q + 4, c0 : c0 + BLOCK].rearrange("g r n -> r g n").bitcast(I32),
                )

        def load_block_scales(n):
            load_scales(w_planes[n % PLANE_TILES], blocks[n][1], blocks[n][2])

        def load_block_codes(n):
            words, c0 = blocks[n][0], blocks[n][2]
            nc.sync.dma_start(
                out=w_codes[n][:].bitcast(I32),
                in_=words[:, :, 2 * c0 : 2 * (c0 + BLOCK)].rearrange("g p c -> p g c").bitcast(I32),
            )

        nc.vector.memset(x_planes[:].bitcast(I32), 0)
        nc.vector.memset(w_planes[0][:].bitcast(I32), 0)

        def load_x_codes(i, g0, g1):
            nc.sync.dma_start(
                out=x_codes[i][:, g0:g1, :].bitcast(I32),
                in_=hidden_states_words[g0:g1, :, BLOCK * i : BLOCK * (i + 1)].rearrange("g p c -> p g c").bitcast(I32),
            )

        def load_first_weights(g):
            nc.sync.dma_start(out=w_codes[0][:, g, :].bitcast(I32), in_=wq_words[g][:, 0 : 2 * BLOCK].bitcast(I32))

        load_x_codes(0, 0, 1)
        load_first_weights(0)
        load_scales(x_planes, hidden_states_scales, 0)
        load_block_scales(0)
        load_x_codes(0, 1, PASSES)
        for g in range(1, PASSES):
            load_first_weights(g)
        load_x_codes(1, 0, PASSES)
        load_block_codes(1)

        ratio = ROPE_THETA ** (-2.0 / HEAD)
        ones = keep.tile([P, 4], F32, name="ones")
        nc.vector.memset(ones[:], 1.0)
        per_turn = keep.tile([P, PAIRS], F32, name="per_turn")
        for i in range(4):
            nc.vector.tensor_scalar(
                out=per_turn[:, i : i + 1], in0=ones[:, i : i + 1], scalar1=ratio**i / TWO_PI, scalar2=None, op0=ALU.mult
            )
        for width in (4, 16):
            for k in range(1, 4):
                nc.vector.tensor_scalar(
                    out=per_turn[:, k * width : (k + 1) * width],
                    in0=per_turn[:, 0:width],
                    scalar1=ratio ** (k * width),
                    scalar2=None,
                    op0=ALU.mult,
                )
        halves = (0, 1)
        turns = []
        whole = []
        frac = []
        for half in halves:
            tu = keep.tile([P, 2, 2, PAIRS], F32, name="turns%d" % half)
            wh = keep.tile([P, 2, 2, PAIRS], I32, name="whole%d" % half)
            fr = keep.tile([P, 2, 2, PAIRS], F32, name="frac%d" % half)
            turns.append(tu)
            whole.append(wh)
            frac.append(fr)
        for t in range(TOKEN_TILES):
            tu = turns[t // 2]
            nc.vector.tensor_scalar(
                out=tu[:, t % 2, 0, :], in0=per_turn[:], scalar1=pos[:, t : t + 1], scalar2=None, op0=ALU.mult
            )
            nc.vector.tensor_scalar(
                out=tu[:, t % 2, 1, :], in0=per_turn[:], scalar1=pos[:, t : t + 1], scalar2=0.25, op0=ALU.mult, op1=ALU.add
            )
        for half in halves:
            nc.vector.tensor_copy(out=whole[half][:], in_=turns[half][:])
        for half in halves:
            nc.vector.tensor_tensor(out=frac[half][:], in0=turns[half][:], in1=whole[half][:], op=ALU.subtract)
        for n in LOAD_ORDER[:EARLY_PLANES]:
            nc.vector.memset(w_planes[n][:].bitcast(I32), 0)
        cos_tab = []
        sin_tab = []
        for half in halves:
            trig = keep.tile([P, 2, 3, PAIRS], F32, name="trig%d" % half)
            nc.scalar.activation(out=trig[:, :, 1:3, :], in_=frac[half][:], func=ACTF.Sin, scale=TWO_PI)
            nc.scalar.activation(out=trig[:, :, 0, :], in_=frac[half][:, :, 0, :], func=ACTF.Sin, scale=-TWO_PI)
            ct = keep.tile([P, 2, PAIRS, 2], F32, name="cos_tab%d" % half)
            st = keep.tile([P, 2, PAIRS, 2], F32, name="sin_tab%d" % half)
            nc.vector.tensor_copy(out=ct[:], in_=trig[:, :, 2, :].unsqueeze(3).to_broadcast([P, 2, PAIRS, 2]))
            nc.vector.tensor_copy(out=st[:], in_=trig[:, :, 0:2, :].rearrange("p t k j -> p t j k"))
            cos_tab.append(ct)
            sin_tab.append(st)

        for n in LOAD_ORDER[EARLY_PLANES:]:
            nc.vector.memset(w_planes[n][:].bitcast(I32), 0)

        load_block_scales(LOAD_ORDER[0])
        for n in LOAD_ORDER[1:FRONT_LOADS]:
            load_block_scales(n)
            load_block_codes(n)

        by_head = [P, HEADS, PAIRS, 2]

        def one_pass(acc, n, m, g, first=0, cols=BLOCK):
            nc.tensor.matmul_mx(
                out=acc[:],
                lhsT=x_codes[m // 2][:, g, 2 * P * (m % 2) : 2 * P * (m % 2 + 1)].bitcast(FP4X4),
                lhsT_scale=x_planes[:, g, P * m : P * (m + 1)],
                rhs=w_codes[n][:, g, 2 * first : 2 * (first + cols)].bitcast(FP4X4),
                rhs_scale=w_planes[n % PLANE_TILES][:, g, first : first + cols],
                start=(g == 0),
                stop=(g == PASSES - 1),
            )

        def group(n, m, first=0, cols=BLOCK):
            acc = psum.tile([P, cols], F32, name="acc")
            for g in range(PASSES):
                one_pass(acc, n, m, g, first, cols)
            return acc

        def products(acc, m, t1, t2):
            pairs = acc[:].rearrange("p (h j e) -> p h j e", h=HEADS, e=2)
            nc.vector.tensor_tensor(
                out=t1.rearrange("p (h j e) -> p h j e", h=HEADS, e=2),
                in0=cos_tab[m // 2][:, m % 2, :, :].unsqueeze(1).to_broadcast(by_head),
                in1=pairs,
                op=ALU.mult,
            )
            nc.vector.tensor_tensor(
                out=t2.rearrange("p (h j e) -> p h j e", h=HEADS, e=2),
                in0=sin_tab[m // 2][:, m % 2, :, :].unsqueeze(1).to_broadcast(by_head),
                in1=pairs[:, :, :, ::-1],
                op=ALU.mult,
            )

        def add_and_store(adder, store, n, m, banks, t1, t2, y):
            out_view, oc0 = blocks[n][3], blocks[n][4]
            adder.tensor_tensor(
                out=y.rearrange("p a c -> p (a c)"),
                in0=t1.rearrange("p a c -> p (a c)"),
                in1=t2.rearrange("p a c -> p (a c)"),
                op=ALU.add,
            )
            store.dma_start(
                out=out_view[P * m : P * (m + banks), oc0 : oc0 + BLOCK].rearrange("(a p) c -> p a c", p=P),
                in_=y,
            )

        head_a = psum.tile([P, BLOCK], F32, name="acc")
        head_b = psum.tile([P, BLOCK], F32, name="acc")
        one_pass(head_a, 0, 0, 0)
        one_pass(head_b, 0, 1, 0)
        for g in range(1, PASSES):
            one_pass(head_a, 0, 0, g)
        for g in range(1, PASSES):
            one_pass(head_b, 0, 1, g)
        head_accs = [head_a, head_b]

        def plain(m, first, cols):
            acc = group(rope_blocks, m, first, cols)
            v = work.tile([P, cols], F32, name="v", bufs=VALUE_PIECES)
            nc.scalar.copy(out=v[:], in_=acc[:])
            nc.scalar.dma_start(out=v_out[P * m : P * (m + 1), first : first + cols], in_=v[:])

        bank_count = TOKEN_TILES * rope_blocks
        pair_count = bank_count // 2
        left_to_vector = []
        pair_index = 0
        for n in range(rope_blocks):
            for m0 in (0, 2):
                t1 = work.tile([P, 2, BLOCK], F32, name="t1")
                t2 = work.tile([P, 2, BLOCK], F32, name="t2")
                y = work.tile([P, 2, BLOCK], F32, name="y")
                store = nc.scalar if pair_index < EARLY_STORES else nc.sync
                on_vector = [2 * pair_index + h >= bank_count - VECTOR_ADDS for h in (0, 1)]
                single = pair_index == 0 or pair_index >= pair_count - 2
                if pair_index == REDUCE_PAIR:
                    both = (t1, t2)
                    for h in (0, 1):
                        acc = group(n, m0 + h)
                        products(acc, m0 + h, both[h][:, 0, :], both[h][:, 1, :])
                    nc.vector.tensor_reduce(
                        out=y[:, 0, :], in_=t1[:].rearrange("p k c -> p c k"), axis=mybir.AxisListType.X, op=ALU.add
                    )
                    store.dma_start(out=blocks[n][3][P * m0 : P * (m0 + 1), blocks[n][4] : blocks[n][4] + BLOCK], in_=y[:, 0, :])
                    add_and_store(nc.gpsimd, store, n, m0 + 1, 1, t2[:, 0:1, :], t2[:, 1:2, :], y[:, 1:2, :])
                    plain(0, 0, BLOCK)
                    pair_index += 1
                    continue
                for h in (0, 1):
                    acc = head_accs[h] if pair_index == 0 else group(n, m0 + h)
                    products(acc, m0 + h, t1[:, h, :], t2[:, h, :])
                    one = (store, n, m0 + h, 1, t1[:, h : h + 1, :], t2[:, h : h + 1, :], y[:, h : h + 1, :])
                    if on_vector[h]:
                        left_to_vector.append(one)
                    elif single:
                        add_and_store(nc.gpsimd, *one)
                if not single:
                    add_and_store(nc.gpsimd, store, n, m0, 2, t1[:], t2[:], y[:])
                if pair_index in LOAD_AFTER_PAIR:
                    load_block_scales(LOAD_AFTER_PAIR[pair_index])
                    load_block_codes(LOAD_AFTER_PAIR[pair_index])
                pair_index += 1
            if n in VALUE_AFTER:
                plain(VALUE_AFTER.index(n), 0, BLOCK)

        for m in range(MID_VALUE_TILES, TOKEN_TILES - 1):
            plain(m, 0, BLOCK)
        first = 0
        for cols in LAST_CUT:
            plain(TOKEN_TILES - 1, first, cols)
            first += cols
        for one in left_to_vector:
            add_and_store(nc.vector, *one)
